import numpy as np
import ml_dtypes


def mxq(x, axis, fmt="e4m3"):
    dtype, down = {"e4m3": (ml_dtypes.float8_e4m3fn, 7), "e5m2": (ml_dtypes.float8_e5m2, 14)}[fmt]
    v = np.moveaxis(np.asarray(x, np.float32).astype(ml_dtypes.bfloat16).astype(np.float64), axis, -1)
    blocks = v.reshape(v.shape[:-1] + (-1, 32))
    amax = np.abs(blocks).max(-1, keepdims=True)
    byte = np.maximum(np.where(amax > 0, np.frexp(amax)[1] - 1 + 127, 0) - down, 1)
    scale = np.exp2(byte - 127.0)
    codes = (blocks / scale).astype(np.float32).astype(dtype).astype(np.float64)
    return np.moveaxis((codes * scale).reshape(v.shape), -1, axis)


WIDE = False


def mx_kscale(k):
    if not WIDE:
        return np.ones(k)
    levels = np.array([10, -10, 5, -5, 0])
    if k % 512:
        return np.exp2(np.random.permutation(np.resize(levels, k // 32))).repeat(32)
    a = np.empty((k // 512, 16))
    for p in range(k // 512):
        a[p, :8] = np.random.permutation(np.resize(levels, 8))
        for g in range(8):
            far = levels[np.abs(levels - a[p, g]) >= 10]
            a[p, g + 8] = far[np.random.randint(len(far))]
    return np.exp2(a.ravel()).repeat(32)


BF16 = ml_dtypes.bfloat16


def bf(x):
    return np.asarray(x, np.float32).astype(BF16)


def f64(x):
    return np.asarray(x).astype(np.float64)


N, X_DIM, Y_DIM, HID = 1024, 512, 512, 2048


def setup_inputs():
    s = mx_kscale(X_DIM)
    t, u = mx_kscale(HID), mx_kscale(HID)
    col = 0.6 + 0.6 * np.random.standard_normal(Y_DIM)
    return {
        "x_samples": bf(np.random.standard_normal((N, X_DIM)) * s),
        "y_samples": bf(np.random.standard_normal((N, Y_DIM)) + col),
        "mu_W1": bf(np.random.standard_normal((X_DIM, HID)) / np.sqrt(X_DIM) / s[:, None] * t),
        "mu_b1": bf(np.random.standard_normal(HID) * 0.8 * t),
        "mu_W2": bf(np.random.standard_normal((HID, Y_DIM)) * 1.2 / np.sqrt(HID) / t[:, None]),
        "mu_b2": bf(0.4 + 0.4 * np.random.standard_normal(Y_DIM)),
        "lv_W1": bf(np.random.standard_normal((X_DIM, HID)) / np.sqrt(X_DIM) / s[:, None] * u),
        "lv_b1": bf(np.random.standard_normal(HID) * 0.8 * u),
        "lv_W2": bf(np.random.standard_normal((HID, Y_DIM)) / np.sqrt(HID) / u[:, None]),
        "lv_b2": bf(0.3 + 0.4 * np.random.standard_normal(Y_DIM)),
    }


def reference(x_samples, y_samples, mu_W1, mu_b1, mu_W2, mu_b2, lv_W1, lv_b1, lv_W2, lv_b2):
    x = f64(x_samples)
    y = f64(y_samples)
    xq = mxq(x, 1, "e4m3")
    h_mu = np.maximum((xq @ mxq(f64(mu_W1), 0, "e4m3")) + f64(mu_b1), 0.0)
    mu = (mxq(h_mu, 1, "e4m3") @ mxq(f64(mu_W2), 0, "e4m3")) + f64(mu_b2)
    h_lv = np.maximum((xq @ mxq(f64(lv_W1), 0, "e4m3")) + f64(lv_b1), 0.0)
    logvar = np.tanh((mxq(h_lv, 1, "e4m3") @ mxq(f64(lv_W2), 0, "e4m3")) + f64(lv_b2))
    w = 0.5 * np.exp(-logvar)
    n = x.shape[0]
    pos_row = -(((mu - y) ** 2) * w).sum(axis=1)
    Sy = y.sum(axis=0)
    Sy2 = (y ** 2).sum(axis=0)
    neg_row = -(w * (n * mu ** 2 - 2.0 * mu * Sy + Sy2)).sum(axis=1) / (n * n)
    return pos_row, neg_row

@@ -1,0 +1,452 @@
+from contextlib import ExitStack
+
+import concourse.mybir as mybir
+from concourse.masks import make_identity
+
+N, X_DIM, Y_DIM, HID = 1024, 512, 512, 2048
+FLOPS = 2 * (2 * N * X_DIM * HID + 2 * N * HID * Y_DIM)
+
+F32 = mybir.dt.float32
+BF16 = mybir.dt.bfloat16
+U32 = mybir.dt.uint32
+U8 = mybir.dt.uint8
+FP8X4 = mybir.dt.float8_e4m3fn_x4
+ACT = mybir.ActivationFunctionType
+ALU = mybir.AluOpType
+
+P = 128
+PACK = 4
+K_PASS = P * PACK
+HALF = 512
+N_HALF = N // HALF
+N_G = HID // K_PASS
+N_DT = Y_DIM // P
+LV, MU = 0, 1
+BANK_DT = F32
+
+N_C = 2 * N_G
+NEG_ROW = 32
+
+W1_LEAD = 3
+FRONT_LEAD = 2
+Y_TICK = 2
+GRAM_TICK = 3
+S_TURNS = (5, 6)
+S_LEAD = 3
+HQ_BUFS = 4
+RAW_BUFS = 6
+
+
+def tile_infoncemi_pa_kernel(
+    tc, x_samples, y_samples, mu_W1, mu_b1, mu_W2, mu_b2, lv_W1, lv_b1, lv_W2, lv_b2, out_0, out_1
+):
+    nc = tc.nc
+    W1 = (lv_W1, mu_W1)
+    B1 = (lv_b1, mu_b1)
+    W2 = (lv_W2, mu_W2)
+    B2 = (lv_b2, mu_b2)
+
+    with ExitStack() as ctx:
+        const = ctx.enter_context(tc.tile_pool(name="const", bufs=1))
+        raw = ctx.enter_context(tc.tile_pool(name="raw", bufs=RAW_BUFS))
+        stage = ctx.enter_context(tc.tile_pool(name="stage", bufs=3))
+        keep = ctx.enter_context(tc.tile_pool(name="keep", bufs=1))
+        epi = ctx.enter_context(tc.tile_pool(name="epi", bufs=2))
+        psum = ctx.enter_context(tc.psum_pool(name="psum", bufs=1))
+        ctx.enter_context(tc.manual_schedule())
+
+        ident_f = const.tile([P, P], F32, name="ident_f")
+        make_identity(nc, ident_f[:])
+        scale_col = const.tile([P, 1], F32, name="scale_col")
+        nc.gpsimd.memset(scale_col[:], -0.5)
+        nc.gpsimd.memset(scale_col[NEG_ROW:2 * NEG_ROW, :], -0.5 / N)
+        warm = const.tile([P, 1], F32, name="warm")
+        nc.scalar.activation(out=warm[:], in_=scale_col[:], func=ACT.Exp)
+        ident_b = const.tile([P, P], BF16, name="ident_b")
+        make_identity(nc, ident_b[:])
+        ones_b = const.tile([P, 32], BF16, name="ones_b")
+        nc.gpsimd.memset(ones_b[:], 1.0)
+        fin = const.tile([P, P], F32, name="fin")
+        nc.gpsimd.memset(fin[:], 0.0)
+
+        def load_rows(src_rows, name):
+            if name[0] == "y":
+                t = keep.tile([P, PACK, 512], BF16, name=name)
+            else:
+                t = raw.tile([P, PACK, 512], BF16, name=name, tag="raw")
+            nc.sync.dma_start(out=t[:], in_=src_rows)
+            return t
+
+        def load_samples(src, h, name):
+            return load_rows(src[h * HALF:(h + 1) * HALF, :].rearrange("(a p) k -> p a k", p=P), "%s%d" % (name, h))
+
+        def load_w(kind, hd, g):
+            if kind == "w1":
+                rows = W1[hd][:, g * K_PASS:(g + 1) * K_PASS].rearrange("(p j) c -> p j c", j=PACK)
+            else:
+                rows = W2[hd][g * K_PASS:(g + 1) * K_PASS, :].rearrange("(p j) d -> p j d", j=PACK)
+            return load_rows(rows, "%sraw%d%d" % (kind, hd, g))
+
+        def load_b1(hd):
+            t = const.tile([P, N_G, PACK], BF16, name="b1_%d" % hd)
+            nc.scalar.dma_start(out=t[:], in_=B1[hd].rearrange("(g p t) -> p g t", g=N_G, t=PACK))
+            return t
+
+        def load_b2(hd):
+            t = const.tile([P, N_DT], BF16, name="b2_%d" % hd)
+            with nc.allow_non_contiguous_dma(reason="one bias element to a partition"):
+                nc.scalar.dma_start(out=t[:], in_=B2[hd].rearrange("(c p) -> p c", p=P))
+            return t
+
+        x_sb, y_sb, b1, b2, wraw = {}, {}, {}, {}, {}
+
+        def load(item):
+            if item[0] == "x":
+                x_sb[item[1]] = load_samples(x_samples, item[1], "x_sb")
+            elif item[0] == "y":
+                y_sb[item[1]] = load_samples(y_samples, item[1], "y_sb")
+            elif item[0] == "b1":
+                b1[item[1]] = load_b1(item[1])
+            elif item[0] == "b2":
+                b2[item[1]] = load_b2(item[1])
+            else:
+                wraw[item] = load_w(*item)
+
+        def w_tick(chunk):
+            c = chunk[1] * N_G + chunk[2]
+            return c - W1_LEAD if chunk[0] == "w1" else c
+
+        def last_use(item):
+            if item[0] == "x":
+                return -W1_LEAD
+            return w_tick(item) if w_tick(item) >= 0 else -W1_LEAD
+
+        w_seq = [("w1", LV, c) for c in range(W1_LEAD)]
+        for c in range(N_C):
+            w_seq.append(("w2", c // N_G, c % N_G))
+            if c + W1_LEAD < N_C:
+                w_seq.append(("w1", (c + W1_LEAD) // N_G, (c + W1_LEAD) % N_G))
+        big = [("x", 0)] + w_seq[0:2] + [("x", 1)] + w_seq[2:]
+        load(("b1", LV))
+        for item in big[:RAW_BUFS]:
+            load(item)
+
+        waiting = [None]
+
+        def flush():
+            if waiting[0] is not None:
+                waiting[0]()
+                waiting[0] = None
+
+        def job(copy_fn, quant_fn):
+            copy_fn()
+            flush()
+            waiting[0] = quant_fn
+
+        def copier(eng):
+            return nc.scalar.copy if eng == "s" else nc.vector.tensor_copy
+
+        xg, xc, xs = {}, {}, {}
+
+        def turn_x(h):
+            xg[h] = stage.tile([P, HALF * PACK], BF16, name="xg", tag="wg", align_bytes=64)
+            xg_words = xg[h][:].bitcast(F32).rearrange("p (s u) -> p s u", u=2)
+            for i in range(2):
+                xt = psum.tile([P, 512], F32, name="xt", tag="s1", bufs=3)
+                for a in range(2):
+                    words = x_sb[h][:, 2 * i + a, :].bitcast(F32)
+                    for u in range(2):
+                        nc.tensor.transpose(xt[:, (2 * a + u) * P:(2 * a + u + 1) * P], words[:, u::2], ident_f[:])
+                nc.scalar.copy(
+                    out=xg_words[:, 256 * i:256 * (i + 1), :].rearrange("p (a s) u -> p a s u", a=2),
+                    in_=xt[:].rearrange("p (a u s) -> p a s u", a=2, u=2),
+                )
+
+        def quant_x(h):
+            xc[h] = keep.tile([P, HALF], U32, name="xc%d" % h, align_bytes=64)
+            xs[h] = keep.tile([P, HALF], U8, name="xs%d" % h, align_bytes=64)
+            nc.vector.quantize_mx(out=xc[h][:].bitcast(FP8X4), scales=xs[h][:], in_=xg[h][:])
+
+        wg, wc, ws = {}, {}, {}
+
+        def copy_w(chunk, eng):
+            wg[chunk] = stage.tile([P, 2048], BF16, name="wg", tag="wg", align_bytes=64)
+            if chunk[0] == "w1":
+                copier(eng)(
+                    out=wg[chunk][:].rearrange("p (t m j) -> p t m j", t=PACK, j=PACK),
+                    in_=wraw[chunk][:].rearrange("p j (m t) -> p t m j", t=PACK),
+                )
+            else:
+                copier(eng)(
+                    out=wg[chunk][:].rearrange("p (d j) -> p d j", j=PACK),
+                    in_=wraw[chunk][:].rearrange("p j d -> p d j"),
+                )
+
+        def quant_w(chunk):
+            wc[chunk] = keep.tile([P, 512], U32, name="%sc%d%d" % chunk, align_bytes=64)
+            ws[chunk] = keep.tile([P, 512], U8, name="%ss%d%d" % chunk, align_bytes=64)
+            nc.vector.quantize_mx(out=wc[chunk][:].bitcast(FP8X4), scales=ws[chunk][:], in_=wg[chunk][:])
+
+        hb, hg, hq, acc = {}, {}, {}, {}
+
+        def front(h, c):
+            hd, g = c // N_G, c % N_G
+            hb[h, c] = stage.tile([P, PACK, HALF], BF16, name="hb%d" % h, tag="hb%d" % h, bufs=(FRONT_LEAD + 2, N_C)[h])
+            for t in range(PACK):
+                bank = psum.tile([P, HALF], BANK_DT, name="bank", tag="s1", bufs=3)
+                cols = slice(t * P, (t + 1) * P)
+                nc.tensor.matmul_mx(
+                    out=bank[:],
+                    lhsT=wc["w1", hd, g][:, cols].bitcast(FP8X4), lhsT_scale=ws["w1", hd, g][:, cols],
+                    rhs=xc[h][:].bitcast(FP8X4), rhs_scale=xs[h][:],
+                    start=True, stop=True,
+                )
+                nc.scalar.activation(out=hb[h, c][:, t, :], in_=bank[:], func=ACT.Relu, bias=b1[hd][:, g, t:t + 1], scale=1.0)
+
+        def copy_h(h, c, eng):
+            hg[h, c] = stage.tile([P, HALF * PACK], BF16, name="hg" + eng, tag="hg" + eng, bufs=3, align_bytes=64)
+            copier(eng)(out=hg[h, c][:].rearrange("p (s t) -> p s t", t=PACK), in_=hb[h, c][:].rearrange("p t s -> p s t"))
+
+        def quant_h(h, c):
+            hc = stage.tile([P, HALF], U32, name="hc", tag="hc", bufs=HQ_BUFS, align_bytes=64)
+            hs = stage.tile([P, HALF], U8, name="hs", tag="hs", bufs=HQ_BUFS, align_bytes=64)
+            nc.vector.quantize_mx(out=hc[:].bitcast(FP8X4), scales=hs[:], in_=hg[h, c][:])
+            hq[h, c] = (hc, hs)
+
+        def back(h, c):
+            hd, g = c // N_G, c % N_G
+            if g == 0:
+                tiles = []
+                for dt in range(N_DT):
+                    a = psum.tile([P, HALF], F32, name="acc", tag="acc", bufs=4)
+                    tiles.append(a)
+                acc[hd, h] = tiles
+            hc, hs = hq[h, c]
+            for dt in range(N_DT):
+                cols = slice(dt * P, (dt + 1) * P)
+                nc.tensor.matmul_mx(
+                    out=acc[hd, h][dt][:],
+                    lhsT=wc["w2", hd, g][:, cols].bitcast(FP8X4), lhsT_scale=ws["w2", hd, g][:, cols],
+                    rhs=hc[:].bitcast(FP8X4), rhs_scale=hs[:],
+                    start=(g == 0), stop=(g == N_G - 1),
+                )
+
+        yT = keep.tile([P, N_DT, N], BF16, name="yT")
+        stat = {}
+
+        def turn_y(c, h):
+            yt = psum.tile([P, HALF], BF16, name="yt", tag="s1", bufs=3)
+            for a in range(4):
+                nc.tensor.transpose(yt[:, a * P:(a + 1) * P], y_sb[h][:, a, c * P:(c + 1) * P], ident_b[:])
+            nc.scalar.copy(out=yT[:, c, h * HALF:(h + 1) * HALF], in_=yt[:])
+
+        def y_squares_pe():
+            gram = psum.tile([P, N_DT * P], F32, name="gram", tag="red", bufs=1)
+            stat["gram"] = gram
+            for c in range(N_DT):
+                for i in range(8):
+                    blk = y_sb[i // 4][:, i % 4, c * P:(c + 1) * P]
+                    nc.tensor.matmul(out=gram[:, c * P:(c + 1) * P], lhsT=blk, rhs=blk, start=(i == 0), stop=(i == 7))
+
+        def y_squares_v():
+            gram = stat["gram"]
+            sy2 = const.tile([P, N_DT], F32, name="sy2")
+            for c in range(N_DT):
+                junk = epi.tile([P, P], F32, name="junk", tag="junk")
+                nc.vector.scalar_tensor_tensor(
+                    out=junk[:], in0=gram[:, c * P:(c + 1) * P], scalar=1.0, in1=ident_f[:],
+                    op0=ALU.mult, op1=ALU.mult, accum_out=sy2[:, c:c + 1],
+                )
+            stat["sy2"] = sy2
+
+        def y_sums_pe():
+            sums = psum.tile([P, N_DT * 32], F32, name="sums", tag="red", bufs=1)
+            stat["sums"] = sums
+            for c in range(N_DT):
+                for i in range(8):
+                    blk = y_sb[i // 4][:, i % 4, c * P:(c + 1) * P]
+                    nc.tensor.matmul(out=sums[:, c * 32:(c + 1) * 32], lhsT=blk, rhs=ones_b[:], start=(i == 0), stop=(i == 7))
+
+        def y_sums_v():
+            sums = stat["sums"]
+            mean = const.tile([P, N_DT], F32, name="mean")
+            nc.vector.tensor_scalar(
+                out=mean[:], in0=sums[:].rearrange("p (c n) -> p c n", n=32)[:, :, 0],
+                scalar1=1.0 / N, scalar2=None, op0=ALU.mult,
+            )
+            msq = const.tile([P, N_DT], F32, name="msq")
+            nc.vector.tensor_tensor(out=msq[:], in0=mean[:], in1=mean[:], op=ALU.mult)
+            var = const.tile([P, N_DT], F32, name="var")
+            nc.vector.scalar_tensor_tensor(
+                out=var[:], in0=stat["sy2"][:], scalar=1.0 / N, in1=msq[:], op0=ALU.mult, op1=ALU.subtract
+            )
+            shift = const.tile([P, N_DT], F32, name="shift")
+            nc.vector.tensor_tensor(out=shift[:], in0=b2[MU][:], in1=mean[:], op=ALU.subtract)
+            stat["var"] = var
+            stat["shift"] = shift
+
+        wexp, q2, d1, e1, red = {}, {}, {}, {}, {}
+
+        def lv_tanh(h, dt):
+            if dt == 0:
+                wexp[h] = keep.tile([P, N_DT, HALF], F32, name="wexp%d" % h)
+            nc.scalar.activation(out=wexp[h][:, dt, :], in_=acc[LV, h][dt][:], func=ACT.Tanh, bias=b2[LV][:, dt:dt + 1], scale=1.0)
+
+        def lv_exp(h, dt):
+            nc.scalar.activation(out=wexp[h][:, dt, :], in_=wexp[h][:, dt, :], func=ACT.Exp, scale=-1.0)
+
+        def mu_read_s(h, dt):
+            q2[h, dt] = epi.tile([P, HALF], F32, name="q2", tag="q2", bufs=4)
+            nc.scalar.activation(out=q2[h, dt][:], in_=acc[MU, h][dt][:], func=ACT.Square, bias=stat["shift"][:, dt:dt + 1], scale=1.0)
+
+        def mu_read_v(h, dt):
+            d1[h, dt] = epi.tile([P, HALF], F32, name="d1", tag="d1", bufs=4)
+            nc.vector.scalar_tensor_tensor(
+                out=d1[h, dt][:], in0=acc[MU, h][dt][:], scalar=b2[MU][:, dt:dt + 1], in1=yT[:, dt, h * HALF:(h + 1) * HALF],
+                op0=ALU.add, op1=ALU.subtract,
+            )
+
+        def mu_square(h, dt):
+            e1[h, dt] = epi.tile([P, HALF], F32, name="e1", tag="e1", bufs=3)
+            nc.scalar.activation(out=e1[h, dt][:], in_=d1[h, dt][:], func=ACT.Square)
+
+        def add_over_d(sums, prod, dt):
+            for b in range(HALF // P):
+                nc.tensor.matmul(
+                    out=sums[:, b * P:(b + 1) * P], lhsT=prod[:, b * P:(b + 1) * P], rhs=ident_f[:], is_transpose=True,
+                    start=(dt == 0 and b == 0), stop=(dt == N_DT - 1 and b == HALF // P - 1),
+                )
+
+        def mu_neg(h, dt):
+            if dt == 0:
+                red[h, 1] = psum.tile([P, HALF], F32, name="tneg", tag="s1", bufs=3)
+            p2 = epi.tile([P, HALF], F32, name="p2", tag="p2")
+            nc.vector.scalar_tensor_tensor(
+                out=p2[:], in0=q2[h, dt][:], scalar=stat["var"][:, dt:dt + 1], in1=wexp[h][:, dt, :],
+                op0=ALU.add, op1=ALU.mult,
+            )
+            add_over_d(red[h, 1], p2, dt)
+
+        def mu_pos(h, dt):
+            if dt == 0:
+                red[h, 0] = psum.tile([P, HALF], F32, name="tpos", tag="s1", bufs=3)
+            p1 = epi.tile([P, HALF], F32, name="p1", tag="p1")
+            nc.vector.tensor_tensor(out=p1[:], in0=e1[h, dt][:], in1=wexp[h][:, dt, :], op=ALU.mult)
+            add_over_d(red[h, 0], p1, dt)
+
+        def gather(h, o):
+            first = o * NEG_ROW + h * (HALF // P)
+            nc.vector.tensor_reduce(
+                out=fin[:, first:first + HALF // P], in_=red[h, o][:].rearrange("p (b d) -> p b d", d=P),
+                axis=mybir.AxisListType.X, op=ALU.add,
+            )
+
+        def finish():
+            fin_t = psum.tile([P, P], F32, name="fin_t", tag="red", bufs=1)
+            nc.tensor.transpose(fin_t[:], fin[:], ident_f[:])
+            rows = NEG_ROW + N // P
+            res = epi.tile([rows, P], F32, name="res", tag="res")
+            nc.scalar.activation(out=res[:], in_=fin_t[0:rows, :], func=ACT.Copy, scale=scale_col[0:rows, :])
+            nc.sync.dma_start(out=out_0.rearrange("(r n) -> r n", n=P), in_=res[0:N // P, :])
+            nc.sync.dma_start(out=out_1.rearrange("(r n) -> r n", n=P), in_=res[NEG_ROW:rows, :])
+
+        def h_job(h, c):
+            job(lambda: copy_h(h, c, "v"), lambda: quant_h(h, c))
+
+        def w_job(chunk):
+            job(lambda: copy_w(chunk, "v"), lambda: quant_w(chunk))
+
+        def loads_after(k):
+            for i in range(RAW_BUFS, len(big)):
+                if last_use(big[i - RAW_BUFS]) == k:
+                    load(big[i])
+
+        turn_x(0)
+        w_job(w_seq[0])
+        quant_x(0)
+        flush()
+        front(0, 0)
+        turn_x(1)
+        w_job(w_seq[1])
+        w_job(w_seq[2])
+        front(0, 1)
+        loads_after(-W1_LEAD)
+
+        for c in range(N_C):
+            h_job(0, c)
+            if c == 0:
+                quant_x(1)
+            if c + FRONT_LEAD < N_C:
+                front(1, c)
+                front(0, c + FRONT_LEAD)
+            if c >= 1:
+                back(0, c - 1)
+                if c == N_G:
+                    for dt in range(N_DT):
+                        lv_tanh(0, dt)
+            if c + FRONT_LEAD > N_C:
+                front(1, c - 1)
+            w_job(("w2", c // N_G, c % N_G))
+            if c + W1_LEAD < N_C:
+                w_job(("w1", (c + W1_LEAD) // N_G, (c + W1_LEAD) % N_G))
+            if c == N_G + 1:
+                for dt in range(N_DT):
+                    lv_exp(0, dt)
+            if c == 0:
+                load(("y", 0))
+                load(("y", 1))
+                load(("b2", LV))
+                load(("b1", MU))
+                load(("b2", MU))
+            if Y_TICK <= c < Y_TICK + 4:
+                turn_y(c - Y_TICK, 0)
+                turn_y(c - Y_TICK, 1)
+            if c == GRAM_TICK:
+                y_squares_pe()
+            if c == GRAM_TICK + 1:
+                y_squares_v()
+            if c == GRAM_TICK + 2:
+                y_sums_pe()
+            loads_after(c)
+
+        flush()
+        back(0, N_C - 1)
+        y_sums_v()
+        for j in range(N_C):
+            if j == 1:
+                front(1, N_C - 1)
+            if j not in S_TURNS:
+                copy_h(1, j, "v")
+            if j == 0:
+                for dt in range(N_DT):
+                    mu_read_s(0, dt)
+                    mu_read_v(0, dt)
+            if j < N_DT:
+                mu_square(0, j)
+            if 1 <= j <= N_DT:
+                mu_neg(0, j - 1)
+            if j == N_G:
+                for dt in range(N_DT):
+                    lv_tanh(1, dt)
+            quant_h(1, j)
+            back(1, j)
+            if 1 <= j <= N_DT:
+                mu_pos(0, j - 1)
+            for i in S_TURNS:
+                if max(i - S_LEAD, 0) == j:
+                    copy_h(1, i, "s")
+            if j == N_G + 1:
+                for dt in range(N_DT):
+                    lv_exp(1, dt)
+
+        gather(0, 1)
+        gather(0, 0)
+        for dt in range(N_DT):
+            mu_read_s(1, dt)
+            mu_read_v(1, dt)
+            mu_square(1, dt)
+            mu_neg(1, dt)
+            mu_pos(1, dt)
+        gather(1, 1)
+        gather(1, 0)
+        finish()

@@ -25,12 +25,14 @@ LV, MU = 0, 1
 BANK_DT = F32
 
 N_C = 2 * N_G
+V_READS = ()
+SLIP = 4
+RUN = 4
 NEG_ROW = 32
 
 W1_LEAD = 3
 FRONT_LEAD = 2
 Y_TICK = 2
-GRAM_TICK = 3
 S_TURNS = (5, 6)
 S_LEAD = 3
 HQ_BUFS = 4
@@ -78,7 +80,13 @@ def tile_infoncemi_pa_kernel(
             return t
 
         def load_samples(src, h, name):
-            return load_rows(src[h * HALF:(h + 1) * HALF, :].rearrange("(a p) k -> p a k", p=P), "%s%d" % (name, h))
+            if name[0] == "y":
+                return load_rows(src[h * HALF:(h + 1) * HALF, :].rearrange("(a p) k -> p a k", p=P), "%s%d" % (name, h))
+            t = raw.tile([P, PACK, 512], BF16, name="%s%d" % (name, h), tag="raw")
+            for i in range(2):
+                rows = src[h * HALF + 2 * i * P:h * HALF + 2 * (i + 1) * P, :]
+                nc.sync.dma_start(out=t[:, 2 * i:2 * (i + 1), :], in_=rows.rearrange("(a p) k -> p a k", p=P))
+            return t
 
         def load_w(kind, hd, g):
             if kind == "w1":
@@ -128,8 +136,11 @@ def tile_infoncemi_pa_kernel(
                 w_seq.append(("w1", (c + W1_LEAD) // N_G, (c + W1_LEAD) % N_G))
         big = [("x", 0)] + w_seq[0:2] + [("x", 1)] + w_seq[2:]
         load(("b1", LV))
-        for item in big[:RAW_BUFS]:
+        for item in big[:RAW_BUFS - 1]:
             load(item)
+        load(("y", 0))
+        load(("y", 1))
+        load(big[RAW_BUFS - 1])
 
         waiting = [None]
 
@@ -152,7 +163,7 @@ def tile_infoncemi_pa_kernel(
             xg[h] = stage.tile([P, HALF * PACK], BF16, name="xg", tag="wg", align_bytes=64)
             xg_words = xg[h][:].bitcast(F32).rearrange("p (s u) -> p s u", u=2)
             for i in range(2):
-                xt = psum.tile([P, 512], F32, name="xt", tag="s1", bufs=3)
+                xt = psum.tile([P, 512], F32, name="xt", tag="s1", bufs=4)
                 for a in range(2):
                     words = x_sb[h][:, 2 * i + a, :].bitcast(F32)
                     for u in range(2):
@@ -178,8 +189,8 @@ def tile_infoncemi_pa_kernel(
                 )
             else:
                 copier(eng)(
-                    out=wg[chunk][:].rearrange("p (d j) -> p d j", j=PACK),
-                    in_=wraw[chunk][:].rearrange("p j d -> p d j"),
+                    out=wg[chunk][:].rearrange("p (c i j) -> p c j i", i=RUN, j=PACK),
+                    in_=wraw[chunk][:].rearrange("p j (c i) -> p c j i", i=RUN),
                 )
 
         def quant_w(chunk):
@@ -189,11 +200,19 @@ def tile_infoncemi_pa_kernel(
 
         hb, hg, hq, acc = {}, {}, {}, {}
 
+        slipped = []
+
+        def slip(count):
+            for i in range(min(count, len(slipped))):
+                out, lhsT, rhs, start, stop = slipped[i]
+                nc.tensor.matmul(out=out, lhsT=lhsT, rhs=rhs, start=start, stop=stop)
+            slipped[0:count] = []
+
         def front(h, c):
             hd, g = c // N_G, c % N_G
             hb[h, c] = stage.tile([P, PACK, HALF], BF16, name="hb%d" % h, tag="hb%d" % h, bufs=(FRONT_LEAD + 2, N_C)[h])
             for t in range(PACK):
-                bank = psum.tile([P, HALF], BANK_DT, name="bank", tag="s1", bufs=3)
+                bank = psum.tile([P, HALF], BANK_DT, name="bank", tag="s1", bufs=4)
                 cols = slice(t * P, (t + 1) * P)
                 nc.tensor.matmul_mx(
                     out=bank[:],
@@ -201,11 +220,20 @@ def tile_infoncemi_pa_kernel(
                     rhs=xc[h][:].bitcast(FP8X4), rhs_scale=xs[h][:],
                     start=True, stop=True,
                 )
-                nc.scalar.activation(out=hb[h, c][:, t, :], in_=bank[:], func=ACT.Relu, bias=b1[hd][:, g, t:t + 1], scale=1.0)
+                slip(SLIP)
+                if h == 1 and t == 0 and c in V_READS:
+                    nc.vector.tensor_scalar(
+                        out=hb[h, c][:, t, :], in0=bank[:], scalar1=b1[hd][:, g, t:t + 1], scalar2=0.0, op0=ALU.add, op1=ALU.max
+                    )
+                else:
+                    nc.scalar.activation(out=hb[h, c][:, t, :], in_=bank[:], func=ACT.Relu, bias=b1[hd][:, g, t:t + 1], scale=1.0)
 
         def copy_h(h, c, eng):
             hg[h, c] = stage.tile([P, HALF * PACK], BF16, name="hg" + eng, tag="hg" + eng, bufs=3, align_bytes=64)
-            copier(eng)(out=hg[h, c][:].rearrange("p (s t) -> p s t", t=PACK), in_=hb[h, c][:].rearrange("p t s -> p s t"))
+            copier(eng)(
+                out=hg[h, c][:].rearrange("p (c i t) -> p c t i", i=RUN, t=PACK),
+                in_=hb[h, c][:].rearrange("p t (c i) -> p c t i", i=RUN),
+            )
 
         def quant_h(h, c):
             hc = stage.tile([P, HALF], U32, name="hc", tag="hc", bufs=HQ_BUFS, align_bytes=64)
@@ -235,20 +263,21 @@ def tile_infoncemi_pa_kernel(
         stat = {}
 
         def turn_y(c, h):
-            yt = psum.tile([P, HALF], BF16, name="yt", tag="s1", bufs=3)
+            yt = psum.tile([P, HALF], BF16, name="yt", tag="s1", bufs=4)
             for a in range(4):
                 nc.tensor.transpose(yt[:, a * P:(a + 1) * P], y_sb[h][:, a, c * P:(c + 1) * P], ident_b[:])
             nc.scalar.copy(out=yT[:, c, h * HALF:(h + 1) * HALF], in_=yt[:])
 
         def y_squares_pe():
-            gram = psum.tile([P, N_DT * P], F32, name="gram", tag="red", bufs=1)
+            gram = psum.tile([P, N_DT * P], F32, name="gram", tag="acc", bufs=4)
             stat["gram"] = gram
             for c in range(N_DT):
                 for i in range(8):
                     blk = y_sb[i // 4][:, i % 4, c * P:(c + 1) * P]
-                    nc.tensor.matmul(out=gram[:, c * P:(c + 1) * P], lhsT=blk, rhs=blk, start=(i == 0), stop=(i == 7))
+                    slipped.append((gram[:, c * P:(c + 1) * P], blk, blk, i == 0, i == 7))
 
         def y_squares_v():
+            assert len(slipped) == 0
             gram = stat["gram"]
             sy2 = const.tile([P, N_DT], F32, name="sy2")
             for c in range(N_DT):
@@ -260,14 +289,15 @@ def tile_infoncemi_pa_kernel(
             stat["sy2"] = sy2
 
         def y_sums_pe():
-            sums = psum.tile([P, N_DT * 32], F32, name="sums", tag="red", bufs=1)
+            sums = psum.tile([P, N_DT * 32], F32, name="sums", tag="acc", bufs=4)
             stat["sums"] = sums
             for c in range(N_DT):
                 for i in range(8):
                     blk = y_sb[i // 4][:, i % 4, c * P:(c + 1) * P]
-                    nc.tensor.matmul(out=sums[:, c * 32:(c + 1) * 32], lhsT=blk, rhs=ones_b[:], start=(i == 0), stop=(i == 7))
+                    slipped.append((sums[:, c * 32:(c + 1) * 32], blk, ones_b[:], i == 0, i == 7))
 
         def y_sums_v():
+            assert len(slipped) == 0
             sums = stat["sums"]
             mean = const.tile([P, N_DT], F32, name="mean")
             nc.vector.tensor_scalar(
@@ -319,7 +349,7 @@ def tile_infoncemi_pa_kernel(
 
         def mu_neg(h, dt):
             if dt == 0:
-                red[h, 1] = psum.tile([P, HALF], F32, name="tneg", tag="s1", bufs=3)
+                red[h, 1] = psum.tile([P, HALF], F32, name="tneg", tag="s1", bufs=4)
             p2 = epi.tile([P, HALF], F32, name="p2", tag="p2")
             nc.vector.scalar_tensor_tensor(
                 out=p2[:], in0=q2[h, dt][:], scalar=stat["var"][:, dt:dt + 1], in1=wexp[h][:, dt, :],
@@ -329,10 +359,18 @@ def tile_infoncemi_pa_kernel(
 
         def mu_pos(h, dt):
             if dt == 0:
-                red[h, 0] = psum.tile([P, HALF], F32, name="tpos", tag="s1", bufs=3)
+                red[h, 0] = psum.tile([P, HALF], F32, name="tpos", tag="s1", bufs=4)
             p1 = epi.tile([P, HALF], F32, name="p1", tag="p1")
             nc.vector.tensor_tensor(out=p1[:], in0=e1[h, dt][:], in1=wexp[h][:, dt, :], op=ALU.mult)
             add_over_d(red[h, 0], p1, dt)
+
+        def gather_s(h, o):
+            first = o * NEG_ROW + h * (HALF // P)
+            for b in range(HALF // P):
+                junk = epi.tile([P, P], F32, name="junk_s", tag="junk_s")
+                nc.scalar.activation(
+                    out=junk[:], in_=red[h, o][:, b * P:(b + 1) * P], func=ACT.Copy, accum_out=fin[:, first + b:first + b + 1]
+                )
 
         def gather(h, o):
             first = o * NEG_ROW + h * (HALF // P)
@@ -342,7 +380,7 @@ def tile_infoncemi_pa_kernel(
             )
 
         def finish():
-            fin_t = psum.tile([P, P], F32, name="fin_t", tag="red", bufs=1)
+            fin_t = psum.tile([P, P], F32, name="fin_t", tag="s1", bufs=4)
             nc.tensor.transpose(fin_t[:], fin[:], ident_f[:])
             rows = NEG_ROW + N // P
             res = epi.tile([rows, P], F32, name="res", tag="res")
@@ -376,10 +414,18 @@ def tile_infoncemi_pa_kernel(
             h_job(0, c)
             if c == 0:
                 quant_x(1)
+                y_squares_pe()
+            if c == 1:
+                y_squares_v()
+                y_sums_pe()
+            if c == 2:
+                y_sums_v()
             if c + FRONT_LEAD < N_C:
                 front(1, c)
                 front(0, c + FRONT_LEAD)
-            if c >= 1:
+            if c == 2:
+                back(0, 0)
+            if c >= 2:
                 back(0, c - 1)
                 if c == N_G:
                     for dt in range(N_DT):
@@ -393,25 +439,16 @@ def tile_infoncemi_pa_kernel(
                 for dt in range(N_DT):
                     lv_exp(0, dt)
             if c == 0:
-                load(("y", 0))
-                load(("y", 1))
                 load(("b2", LV))
                 load(("b1", MU))
                 load(("b2", MU))
             if Y_TICK <= c < Y_TICK + 4:
                 turn_y(c - Y_TICK, 0)
                 turn_y(c - Y_TICK, 1)
-            if c == GRAM_TICK:
-                y_squares_pe()
-            if c == GRAM_TICK + 1:
-                y_squares_v()
-            if c == GRAM_TICK + 2:
-                y_sums_pe()
             loads_after(c)
 
         flush()
         back(0, N_C - 1)
-        y_sums_v()
         for j in range(N_C):
             if j == 1:
                 front(1, N_C - 1)
@@ -439,14 +476,16 @@ def tile_infoncemi_pa_kernel(
                 for dt in range(N_DT):
                     lv_exp(1, dt)
 
-        gather(0, 1)
-        gather(0, 0)
-        for dt in range(N_DT):
-            mu_read_s(1, dt)
-            mu_read_v(1, dt)
-            mu_square(1, dt)
-            mu_neg(1, dt)
-            mu_pos(1, dt)
-        gather(1, 1)
+        gather_s(0, 1)
+        gather_s(0, 0)
+        for dt in range(N_DT + 1):
+            if dt < N_DT:
+                mu_read_s(1, dt)
+                mu_read_v(1, dt)
+                mu_square(1, dt)
+            if dt >= 1:
+                mu_neg(1, dt - 1)
+                mu_pos(1, dt - 1)
+        gather_s(1, 1)
         gather(1, 0)
         finish()

@@ -25,7 +25,7 @@ LV, MU = 0, 1
 BANK_DT = F32
 
 N_C = 2 * N_G
-V_READS = ()
+V_READS = (0, 1, 2, 3, 4, 5, 6, 7)
 SLIP = 4
 RUN = 4
 NEG_ROW = 32
@@ -221,7 +221,7 @@ def tile_infoncemi_pa_kernel(
                     start=True, stop=True,
                 )
                 slip(SLIP)
-                if h == 1 and t == 0 and c in V_READS:
+                if h == 1 and t % 2 == 0 and c in V_READS:
                     nc.vector.tensor_scalar(
                         out=hb[h, c][:, t, :], in0=bank[:], scalar1=b1[hd][:, g, t:t + 1], scalar2=0.0, op0=ALU.add, op1=ALU.max
                     )

from contextlib import ExitStack

import concourse.mybir as mybir
from concourse.masks import make_identity

N, X_DIM, Y_DIM, HID = 1024, 512, 512, 2048
FLOPS = 2 * (2 * N * X_DIM * HID + 2 * N * HID * Y_DIM)

F32 = mybir.dt.float32
BF16 = mybir.dt.bfloat16
U32 = mybir.dt.uint32
U8 = mybir.dt.uint8
FP8X4 = mybir.dt.float8_e4m3fn_x4
ACT = mybir.ActivationFunctionType
ALU = mybir.AluOpType

P = 128
PACK = 4
K_PASS = P * PACK
HALF = 512
N_HALF = N // HALF
N_G = HID // K_PASS
N_DT = Y_DIM // P
LV, MU = 0, 1
BANK_DT = F32

N_C = 2 * N_G
V_READS = (0, 1, 2, 3, 4, 5, 6, 7)
SLIP = 4
RUN = 4
NEG_ROW = 32

W1_LEAD = 3
FRONT_LEAD = 2
Y_TICK = 2
S_TURNS = (5, 6)
S_LEAD = 3
HQ_BUFS = 4
RAW_BUFS = 6


def tile_infoncemi_pa_kernel(
    tc, x_samples, y_samples, mu_W1, mu_b1, mu_W2, mu_b2, lv_W1, lv_b1, lv_W2, lv_b2, out_0, out_1
):
    nc = tc.nc
    W1 = (lv_W1, mu_W1)
    B1 = (lv_b1, mu_b1)
    W2 = (lv_W2, mu_W2)
    B2 = (lv_b2, mu_b2)

    with ExitStack() as ctx:
        const = ctx.enter_context(tc.tile_pool(name="const", bufs=1))
        raw = ctx.enter_context(tc.tile_pool(name="raw", bufs=RAW_BUFS))
        stage = ctx.enter_context(tc.tile_pool(name="stage", bufs=3))
        keep = ctx.enter_context(tc.tile_pool(name="keep", bufs=1))
        epi = ctx.enter_context(tc.tile_pool(name="epi", bufs=2))
        psum = ctx.enter_context(tc.psum_pool(name="psum", bufs=1))
        ctx.enter_context(tc.manual_schedule())

        ident_f = const.tile([P, P], F32, name="ident_f")
        make_identity(nc, ident_f[:])
        scale_col = const.tile([P, 1], F32, name="scale_col")
        nc.gpsimd.memset(scale_col[:], -0.5)
        nc.gpsimd.memset(scale_col[NEG_ROW:2 * NEG_ROW, :], -0.5 / N)
        warm = const.tile([P, 1], F32, name="warm")
        nc.scalar.activation(out=warm[:], in_=scale_col[:], func=ACT.Exp)
        ident_b = const.tile([P, P], BF16, name="ident_b")
        make_identity(nc, ident_b[:])
        ones_b = const.tile([P, 32], BF16, name="ones_b")
        nc.gpsimd.memset(ones_b[:], 1.0)
        fin = const.tile([P, P], F32, name="fin")
        nc.gpsimd.memset(fin[:], 0.0)

        def load_rows(src_rows, name):
            if name[0] == "y":
                t = keep.tile([P, PACK, 512], BF16, name=name)
            else:
                t = raw.tile([P, PACK, 512], BF16, name=name, tag="raw")
            nc.sync.dma_start(out=t[:], in_=src_rows)
            return t

        def load_samples(src, h, name):
            if name[0] == "y":
                return load_rows(src[h * HALF:(h + 1) * HALF, :].rearrange("(a p) k -> p a k", p=P), "%s%d" % (name, h))
            t = raw.tile([P, PACK, 512], BF16, name="%s%d" % (name, h), tag="raw")
            for i in range(2):
                rows = src[h * HALF + 2 * i * P:h * HALF + 2 * (i + 1) * P, :]
                nc.sync.dma_start(out=t[:, 2 * i:2 * (i + 1), :], in_=rows.rearrange("(a p) k -> p a k", p=P))
            return t

        def load_w(kind, hd, g):
            if kind == "w1":
                rows = W1[hd][:, g * K_PASS:(g + 1) * K_PASS].rearrange("(p j) c -> p j c", j=PACK)
            else:
                rows = W2[hd][g * K_PASS:(g + 1) * K_PASS, :].rearrange("(p j) d -> p j d", j=PACK)
            return load_rows(rows, "%sraw%d%d" % (kind, hd, g))

        def load_b1(hd):
            t = const.tile([P, N_G, PACK], BF16, name="b1_%d" % hd)
            nc.scalar.dma_start(out=t[:], in_=B1[hd].rearrange("(g p t) -> p g t", g=N_G, t=PACK))
            return t

        def load_b2(hd):
            t = const.tile([P, N_DT], BF16, name="b2_%d" % hd)
            with nc.allow_non_contiguous_dma(reason="one bias element to a partition"):
                nc.scalar.dma_start(out=t[:], in_=B2[hd].rearrange("(c p) -> p c", p=P))
            return t

        x_sb, y_sb, b1, b2, wraw = {}, {}, {}, {}, {}

        def load(item):
            if item[0] == "x":
                x_sb[item[1]] = load_samples(x_samples, item[1], "x_sb")
            elif item[0] == "y":
                y_sb[item[1]] = load_samples(y_samples, item[1], "y_sb")
            elif item[0] == "b1":
                b1[item[1]] = load_b1(item[1])
            elif item[0] == "b2":
                b2[item[1]] = load_b2(item[1])
            else:
                wraw[item] = load_w(*item)

        def w_tick(chunk):
            c = chunk[1] * N_G + chunk[2]
            return c - W1_LEAD if chunk[0] == "w1" else c

        def last_use(item):
            if item[0] == "x":
                return -W1_LEAD
            return w_tick(item) if w_tick(item) >= 0 else -W1_LEAD

        w_seq = [("w1", LV, c) for c in range(W1_LEAD)]
        for c in range(N_C):
            w_seq.append(("w2", c // N_G, c % N_G))
            if c + W1_LEAD < N_C:
                w_seq.append(("w1", (c + W1_LEAD) // N_G, (c + W1_LEAD) % N_G))
        big = [("x", 0)] + w_seq[0:2] + [("x", 1)] + w_seq[2:]
        load(("b1", LV))
        for item in big[:RAW_BUFS - 1]:
            load(item)
        load(("y", 0))
        load(("y", 1))
        load(big[RAW_BUFS - 1])

        waiting = [None]

        def flush():
            if waiting[0] is not None:
                waiting[0]()
                waiting[0] = None

        def job(copy_fn, quant_fn):
            copy_fn()
            flush()
            waiting[0] = quant_fn

        def copier(eng):
            return nc.scalar.copy if eng == "s" else nc.vector.tensor_copy

        xg, xc, xs = {}, {}, {}

        def turn_x(h):
            xg[h] = stage.tile([P, HALF * PACK], BF16, name="xg", tag="wg", align_bytes=64)
            xg_words = xg[h][:].bitcast(F32).rearrange("p (s u) -> p s u", u=2)
            for i in range(2):
                xt = psum.tile([P, 512], F32, name="xt", tag="s1", bufs=4)
                for a in range(2):
                    words = x_sb[h][:, 2 * i + a, :].bitcast(F32)
                    for u in range(2):
                        nc.tensor.transpose(xt[:, (2 * a + u) * P:(2 * a + u + 1) * P], words[:, u::2], ident_f[:])
                nc.scalar.copy(
                    out=xg_words[:, 256 * i:256 * (i + 1), :].rearrange("p (a s) u -> p a s u", a=2),
                    in_=xt[:].rearrange("p (a u s) -> p a s u", a=2, u=2),
                )

        def quant_x(h):
            xc[h] = keep.tile([P, HALF], U32, name="xc%d" % h, align_bytes=64)
            xs[h] = keep.tile([P, HALF], U8, name="xs%d" % h, align_bytes=64)
            nc.vector.quantize_mx(out=xc[h][:].bitcast(FP8X4), scales=xs[h][:], in_=xg[h][:])

        wg, wc, ws = {}, {}, {}

        def copy_w(chunk, eng):
            wg[chunk] = stage.tile([P, 2048], BF16, name="wg", tag="wg", align_bytes=64)
            if chunk[0] == "w1":
                copier(eng)(
                    out=wg[chunk][:].rearrange("p (t m j) -> p t m j", t=PACK, j=PACK),
                    in_=wraw[chunk][:].rearrange("p j (m t) -> p t m j", t=PACK),
                )
            else:
                copier(eng)(
                    out=wg[chunk][:].rearrange("p (c i j) -> p c j i", i=RUN, j=PACK),
                    in_=wraw[chunk][:].rearrange("p j (c i) -> p c j i", i=RUN),
                )

        def quant_w(chunk):
            wc[chunk] = keep.tile([P, 512], U32, name="%sc%d%d" % chunk, align_bytes=64)
            ws[chunk] = keep.tile([P, 512], U8, name="%ss%d%d" % chunk, align_bytes=64)
            nc.vector.quantize_mx(out=wc[chunk][:].bitcast(FP8X4), scales=ws[chunk][:], in_=wg[chunk][:])

        hb, hg, hq, acc = {}, {}, {}, {}

        slipped = []

        def slip(count):
            for i in range(min(count, len(slipped))):
                out, lhsT, rhs, start, stop = slipped[i]
                nc.tensor.matmul(out=out, lhsT=lhsT, rhs=rhs, start=start, stop=stop)
            slipped[0:count] = []

        def front(h, c):
            hd, g = c // N_G, c % N_G
            hb[h, c] = stage.tile([P, PACK, HALF], BF16, name="hb%d" % h, tag="hb%d" % h, bufs=(FRONT_LEAD + 2, N_C)[h])
            for t in range(PACK):
                bank = psum.tile([P, HALF], BANK_DT, name="bank", tag="s1", bufs=4)
                cols = slice(t * P, (t + 1) * P)
                nc.tensor.matmul_mx(
                    out=bank[:],
                    lhsT=wc["w1", hd, g][:, cols].bitcast(FP8X4), lhsT_scale=ws["w1", hd, g][:, cols],
                    rhs=xc[h][:].bitcast(FP8X4), rhs_scale=xs[h][:],
                    start=True, stop=True,
                )
                slip(SLIP)
                if h == 1 and t % 2 == 0 and c in V_READS:
                    nc.vector.tensor_scalar(
                        out=hb[h, c][:, t, :], in0=bank[:], scalar1=b1[hd][:, g, t:t + 1], scalar2=0.0, op0=ALU.add, op1=ALU.max
                    )
                else:
                    nc.scalar.activation(out=hb[h, c][:, t, :], in_=bank[:], func=ACT.Relu, bias=b1[hd][:, g, t:t + 1], scale=1.0)

        def copy_h(h, c, eng):
            hg[h, c] = stage.tile([P, HALF * PACK], BF16, name="hg" + eng, tag="hg" + eng, bufs=3, align_bytes=64)
            copier(eng)(
                out=hg[h, c][:].rearrange("p (c i t) -> p c t i", i=RUN, t=PACK),
                in_=hb[h, c][:].rearrange("p t (c i) -> p c t i", i=RUN),
            )

        def quant_h(h, c):
            hc = stage.tile([P, HALF], U32, name="hc", tag="hc", bufs=HQ_BUFS, align_bytes=64)
            hs = stage.tile([P, HALF], U8, name="hs", tag="hs", bufs=HQ_BUFS, align_bytes=64)
            nc.vector.quantize_mx(out=hc[:].bitcast(FP8X4), scales=hs[:], in_=hg[h, c][:])
            hq[h, c] = (hc, hs)

        def back(h, c):
            hd, g = c // N_G, c % N_G
            if g == 0:
                tiles = []
                for dt in range(N_DT):
                    a = psum.tile([P, HALF], F32, name="acc", tag="acc", bufs=4)
                    tiles.append(a)
                acc[hd, h] = tiles
            hc, hs = hq[h, c]
            for dt in range(N_DT):
                cols = slice(dt * P, (dt + 1) * P)
                nc.tensor.matmul_mx(
                    out=acc[hd, h][dt][:],
                    lhsT=wc["w2", hd, g][:, cols].bitcast(FP8X4), lhsT_scale=ws["w2", hd, g][:, cols],
                    rhs=hc[:].bitcast(FP8X4), rhs_scale=hs[:],
                    start=(g == 0), stop=(g == N_G - 1),
                )

        yT = keep.tile([P, N_DT, N], BF16, name="yT")
        stat = {}

        def turn_y(c, h):
            yt = psum.tile([P, HALF], BF16, name="yt", tag="s1", bufs=4)
            for a in range(4):
                nc.tensor.transpose(yt[:, a * P:(a + 1) * P], y_sb[h][:, a, c * P:(c + 1) * P], ident_b[:])
            nc.scalar.copy(out=yT[:, c, h * HALF:(h + 1) * HALF], in_=yt[:])

        def y_squares_pe():
            gram = psum.tile([P, N_DT * P], F32, name="gram", tag="acc", bufs=4)
            stat["gram"] = gram
            for c in range(N_DT):
                for i in range(8):
                    blk = y_sb[i // 4][:, i % 4, c * P:(c + 1) * P]
                    slipped.append((gram[:, c * P:(c + 1) * P], blk, blk, i == 0, i == 7))

        def y_squares_v():
            assert len(slipped) == 0
            gram = stat["gram"]
            sy2 = const.tile([P, N_DT], F32, name="sy2")
            for c in range(N_DT):
                junk = epi.tile([P, P], F32, name="junk", tag="junk")
                nc.vector.scalar_tensor_tensor(
                    out=junk[:], in0=gram[:, c * P:(c + 1) * P], scalar=1.0, in1=ident_f[:],
                    op0=ALU.mult, op1=ALU.mult, accum_out=sy2[:, c:c + 1],
                )
            stat["sy2"] = sy2

        def y_sums_pe():
            sums = psum.tile([P, N_DT * 32], F32, name="sums", tag="acc", bufs=4)
            stat["sums"] = sums
            for c in range(N_DT):
                for i in range(8):
                    blk = y_sb[i // 4][:, i % 4, c * P:(c + 1) * P]
                    slipped.append((sums[:, c * 32:(c + 1) * 32], blk, ones_b[:], i == 0, i == 7))

        def y_sums_v():
            assert len(slipped) == 0
            sums = stat["sums"]
            mean = const.tile([P, N_DT], F32, name="mean")
            nc.vector.tensor_scalar(
                out=mean[:], in0=sums[:].rearrange("p (c n) -> p c n", n=32)[:, :, 0],
                scalar1=1.0 / N, scalar2=None, op0=ALU.mult,
            )
            msq = const.tile([P, N_DT], F32, name="msq")
            nc.vector.tensor_tensor(out=msq[:], in0=mean[:], in1=mean[:], op=ALU.mult)
            var = const.tile([P, N_DT], F32, name="var")
            nc.vector.scalar_tensor_tensor(
                out=var[:], in0=stat["sy2"][:], scalar=1.0 / N, in1=msq[:], op0=ALU.mult, op1=ALU.subtract
            )
            shift = const.tile([P, N_DT], F32, name="shift")
            nc.vector.tensor_tensor(out=shift[:], in0=b2[MU][:], in1=mean[:], op=ALU.subtract)
            stat["var"] = var
            stat["shift"] = shift

        wexp, q2, d1, e1, red = {}, {}, {}, {}, {}

        def lv_tanh(h, dt):
            if dt == 0:
                wexp[h] = keep.tile([P, N_DT, HALF], F32, name="wexp%d" % h)
            nc.scalar.activation(out=wexp[h][:, dt, :], in_=acc[LV, h][dt][:], func=ACT.Tanh, bias=b2[LV][:, dt:dt + 1], scale=1.0)

        def lv_exp(h, dt):
            nc.scalar.activation(out=wexp[h][:, dt, :], in_=wexp[h][:, dt, :], func=ACT.Exp, scale=-1.0)

        def mu_read_s(h, dt):
            q2[h, dt] = epi.tile([P, HALF], F32, name="q2", tag="q2", bufs=4)
            nc.scalar.activation(out=q2[h, dt][:], in_=acc[MU, h][dt][:], func=ACT.Square, bias=stat["shift"][:, dt:dt + 1], scale=1.0)

        def mu_read_v(h, dt):
            d1[h, dt] = epi.tile([P, HALF], F32, name="d1", tag="d1", bufs=4)
            nc.vector.scalar_tensor_tensor(
                out=d1[h, dt][:], in0=acc[MU, h][dt][:], scalar=b2[MU][:, dt:dt + 1], in1=yT[:, dt, h * HALF:(h + 1) * HALF],
                op0=ALU.add, op1=ALU.subtract,
            )

        def mu_square(h, dt):
            e1[h, dt] = epi.tile([P, HALF], F32, name="e1", tag="e1", bufs=3)
            nc.scalar.activation(out=e1[h, dt][:], in_=d1[h, dt][:], func=ACT.Square)

        def add_over_d(sums, prod, dt):
            for b in range(HALF // P):
                nc.tensor.matmul(
                    out=sums[:, b * P:(b + 1) * P], lhsT=prod[:, b * P:(b + 1) * P], rhs=ident_f[:], is_transpose=True,
                    start=(dt == 0 and b == 0), stop=(dt == N_DT - 1 and b == HALF // P - 1),
                )

        def mu_neg(h, dt):
            if dt == 0:
                red[h, 1] = psum.tile([P, HALF], F32, name="tneg", tag="s1", bufs=4)
            p2 = epi.tile([P, HALF], F32, name="p2", tag="p2")
            nc.vector.scalar_tensor_tensor(
                out=p2[:], in0=q2[h, dt][:], scalar=stat["var"][:, dt:dt + 1], in1=wexp[h][:, dt, :],
                op0=ALU.add, op1=ALU.mult,
            )
            add_over_d(red[h, 1], p2, dt)

        def mu_pos(h, dt):
            if dt == 0:
                red[h, 0] = psum.tile([P, HALF], F32, name="tpos", tag="s1", bufs=4)
            p1 = epi.tile([P, HALF], F32, name="p1", tag="p1")
            nc.vector.tensor_tensor(out=p1[:], in0=e1[h, dt][:], in1=wexp[h][:, dt, :], op=ALU.mult)
            add_over_d(red[h, 0], p1, dt)

        def gather_s(h, o):
            first = o * NEG_ROW + h * (HALF // P)
            for b in range(HALF // P):
                junk = epi.tile([P, P], F32, name="junk_s", tag="junk_s")
                nc.scalar.activation(
                    out=junk[:], in_=red[h, o][:, b * P:(b + 1) * P], func=ACT.Copy, accum_out=fin[:, first + b:first + b + 1]
                )

        def gather(h, o):
            first = o * NEG_ROW + h * (HALF // P)
            nc.vector.tensor_reduce(
                out=fin[:, first:first + HALF // P], in_=red[h, o][:].rearrange("p (b d) -> p b d", d=P),
                axis=mybir.AxisListType.X, op=ALU.add,
            )

        def finish():
            fin_t = psum.tile([P, P], F32, name="fin_t", tag="s1", bufs=4)
            nc.tensor.transpose(fin_t[:], fin[:], ident_f[:])
            rows = NEG_ROW + N // P
            res = epi.tile([rows, P], F32, name="res", tag="res")
            nc.scalar.activation(out=res[:], in_=fin_t[0:rows, :], func=ACT.Copy, scale=scale_col[0:rows, :])
            nc.sync.dma_start(out=out_0.rearrange("(r n) -> r n", n=P), in_=res[0:N // P, :])
            nc.sync.dma_start(out=out_1.rearrange("(r n) -> r n", n=P), in_=res[NEG_ROW:rows, :])

        def h_job(h, c):
            job(lambda: copy_h(h, c, "v"), lambda: quant_h(h, c))

        def w_job(chunk):
            job(lambda: copy_w(chunk, "v"), lambda: quant_w(chunk))

        def loads_after(k):
            for i in range(RAW_BUFS, len(big)):
                if last_use(big[i - RAW_BUFS]) == k:
                    load(big[i])

        turn_x(0)
        w_job(w_seq[0])
        quant_x(0)
        flush()
        front(0, 0)
        turn_x(1)
        w_job(w_seq[1])
        w_job(w_seq[2])
        front(0, 1)
        loads_after(-W1_LEAD)

        for c in range(N_C):
            h_job(0, c)
            if c == 0:
                quant_x(1)
                y_squares_pe()
            if c == 1:
                y_squares_v()
                y_sums_pe()
            if c == 2:
                y_sums_v()
            if c + FRONT_LEAD < N_C:
                front(1, c)
                front(0, c + FRONT_LEAD)
            if c == 2:
                back(0, 0)
            if c >= 2:
                back(0, c - 1)
                if c == N_G:
                    for dt in range(N_DT):
                        lv_tanh(0, dt)
            if c + FRONT_LEAD > N_C:
                front(1, c - 1)
            w_job(("w2", c // N_G, c % N_G))
            if c + W1_LEAD < N_C:
                w_job(("w1", (c + W1_LEAD) // N_G, (c + W1_LEAD) % N_G))
            if c == N_G + 1:
                for dt in range(N_DT):
                    lv_exp(0, dt)
            if c == 0:
                load(("b2", LV))
                load(("b1", MU))
                load(("b2", MU))
            if Y_TICK <= c < Y_TICK + 4:
                turn_y(c - Y_TICK, 0)
                turn_y(c - Y_TICK, 1)
            loads_after(c)

        flush()
        back(0, N_C - 1)
        for j in range(N_C):
            if j == 1:
                front(1, N_C - 1)
            if j not in S_TURNS:
                copy_h(1, j, "v")
            if j == 0:
                for dt in range(N_DT):
                    mu_read_s(0, dt)
                    mu_read_v(0, dt)
            if j < N_DT:
                mu_square(0, j)
            if 1 <= j <= N_DT:
                mu_neg(0, j - 1)
            if j == N_G:
                for dt in range(N_DT):
                    lv_tanh(1, dt)
            quant_h(1, j)
            back(1, j)
            if 1 <= j <= N_DT:
                mu_pos(0, j - 1)
            for i in S_TURNS:
                if max(i - S_LEAD, 0) == j:
                    copy_h(1, i, "s")
            if j == N_G + 1:
                for dt in range(N_DT):
                    lv_exp(1, dt)

        gather_s(0, 1)
        gather_s(0, 0)
        for dt in range(N_DT + 1):
            if dt < N_DT:
                mu_read_s(1, dt)
                mu_read_v(1, dt)
                mu_square(1, dt)
            if dt >= 1:
                mu_neg(1, dt - 1)
                mu_pos(1, dt - 1)
        gather_s(1, 1)
        gather(1, 0)
        finish()
